import numpy as np
import ml_dtypes


def mxq(x, axis, fmt="e4m3"):
    dtype, down = {"e4m3": (ml_dtypes.float8_e4m3fn, 7), "e5m2": (ml_dtypes.float8_e5m2, 14)}[fmt]
    v = np.moveaxis(np.asarray(x, np.float32).astype(ml_dtypes.bfloat16).astype(np.float64), axis, -1)
    blocks = v.reshape(v.shape[:-1] + (-1, 32))
    amax = np.abs(blocks).max(-1, keepdims=True)
    byte = np.maximum(np.where(amax > 0, np.frexp(amax)[1] - 1 + 127, 0) - down, 1)
    scale = np.exp2(byte - 127.0)
    codes = (blocks / scale).astype(np.float32).astype(dtype).astype(np.float64)
    return np.moveaxis((codes * scale).reshape(v.shape), -1, axis)


WIDE = False


def mx_kscale(k):
    if not WIDE:
        return np.ones(k)
    levels = np.array([10, -10, 5, -5, 0])
    if k % 512:
        return np.exp2(np.random.permutation(np.resize(levels, k // 32))).repeat(32)
    a = np.empty((k // 512, 16))
    for p in range(k // 512):
        a[p, :8] = np.random.permutation(np.resize(levels, 8))
        for g in range(8):
            far = levels[np.abs(levels - a[p, g]) >= 10]
            a[p, g + 8] = far[np.random.randint(len(far))]
    return np.exp2(a.ravel()).repeat(32)


BF16 = ml_dtypes.bfloat16


def bf(x):
    return np.asarray(x, np.float32).astype(BF16)


def f64(x):
    return np.asarray(x).astype(np.float64)


B, T, E, C, H, XB = 1, 512, 2048, 2048, 16, 512
D = C // H


def decay_mask():
    gamma = 1.0 - 2.0 ** (-5.0 - f64(np.arange(H)))
    idx = np.arange(T)
    diff = idx[:, None] - idx[None, :]
    ex = f64(np.where(diff >= 0, diff, 0))
    return np.where(diff[None] >= 0, gamma[:, None, None] ** ex[None], 0.0)


def setup_inputs():
    s = mx_kscale(T)
    return {"q_rot": bf(np.random.standard_normal((B, T, C)) * 0.4),
            "k_rot": bf(np.random.standard_normal((B, T, C)) * 0.4 * s[None, :, None]),
            "v": bf(np.random.standard_normal((B, T, C)) * 0.5 / s[None, :, None])}


def reference(q_rot, k_rot, v):
    q = f64(q_rot).reshape(B, T, H, D).transpose(0, 2, 1, 3)
    k = f64(k_rot).reshape(B, T, H, D).transpose(0, 2, 1, 3)
    vh = f64(v).reshape(B, T, H, D).transpose(0, 2, 1, 3)
    scores = (q @ k.transpose(0, 1, 3, 2)) * (D ** -0.5)
    sm = scores * decay_mask()[None]
    y = mxq(sm, 3, "e4m3") @ mxq(vh, 2, "e4m3")
    return y.transpose(0, 2, 1, 3).reshape(B, T, C)

@@ -1,0 +1,234 @@
+import math
+from contextlib import ExitStack
+
+import concourse.mybir as mybir
+from concourse.masks import make_identity
+
+BF16 = mybir.dt.bfloat16
+F32 = mybir.dt.float32
+U32 = mybir.dt.uint32
+U8 = mybir.dt.uint8
+FP8X4 = mybir.dt.float8_e4m3fn_x4
+EXP = mybir.ActivationFunctionType.Exp
+MULT = mybir.AluOpType.mult
+
+P = 128
+PACK = 4
+T = 512
+HEADS = 16
+D = 128
+GROUP = 2
+GROUP_COLS = GROUP * D
+V_GROUP = 4
+V_GROUP_COLS = V_GROUP * D
+MASKED = 2.0 ** 30
+RUN = 4
+SM_BUFS = 3
+TABLES_AHEAD = 4
+DECAY_COLS = T + PACK - 1
+
+FLOPS = 2 * 2 * HEADS * T * T * D
+
+
+def tile_multiscaleretention_pb_kernel(tc, q_rot, k_rot, v, out):
+    nc = tc.nc
+    q_view = q_rot.rearrange("b (p c) e -> p (b c) e", c=PACK)
+    k_view = k_rot.rearrange("b (p c) e -> p (b c) e", c=PACK)
+    v_view = v.rearrange("b (p c) e -> p (b c) e", c=PACK)
+    out_view = out.rearrange("b (p c) e -> p (b c) e", c=PACK)
+
+    with ExitStack() as ctx:
+        ctx.enter_context(tc.manual_schedule())
+        keep = ctx.enter_context(tc.tile_pool(name="keep", bufs=1))
+        work = ctx.enter_context(tc.tile_pool(name="work", bufs=3))
+        psum_t = ctx.enter_context(tc.psum_pool(name="psum_t", bufs=2))
+        psum_s = ctx.enter_context(tc.psum_pool(name="psum_s", bufs=4))
+        psum_y = ctx.enter_context(tc.psum_pool(name="psum_y", bufs=2))
+
+        q_sb = []
+        k_sb = []
+        v_sb = []
+        for g in range(HEADS // GROUP):
+            cols = slice(g * GROUP_COLS, (g + 1) * GROUP_COLS)
+            q_g = keep.tile([P, PACK, GROUP_COLS], BF16, name="q_g%d" % g)
+            k_g = keep.tile([P, PACK, GROUP_COLS], BF16, name="k_g%d" % g)
+            nc.sync.dma_start(out=q_g[:], in_=q_view[:, :, cols])
+            nc.sync.dma_start(out=k_g[:], in_=k_view[:, :, cols])
+            q_sb.append(q_g)
+            k_sb.append(k_g)
+            if (g * GROUP) % V_GROUP == 0:
+                first = g * GROUP_COLS
+                v_g = keep.tile([P, PACK, V_GROUP_COLS], BF16, name="v_g%d" % len(v_sb))
+                nc.sync.dma_start(out=v_g[:], in_=v_view[:, :, first : first + V_GROUP_COLS])
+                v_sb.append(v_g)
+
+        distance = keep.tile([P, DECAY_COLS], F32, name="distance")
+        distance_pattern = [[1, DECAY_COLS]]
+        nc.gpsimd.iota(
+            distance[:],
+            pattern=distance_pattern,
+            base=1 - PACK,
+            channel_multiplier=-PACK,
+            allow_small_or_imprecise_dtypes=True,
+        )
+        nc.gpsimd.affine_select(
+            out=distance[:],
+            in_=distance[:],
+            pattern=distance_pattern,
+            compare_op=mybir.AluOpType.is_ge,
+            fill=MASKED,
+            base=1 - PACK,
+            channel_multiplier=-PACK,
+        )
+
+        ident = keep.tile([P, P], BF16, name="ident")
+        make_identity(nc, ident[:])
+
+        sm_tiles = []
+        for i in range(SM_BUFS):
+            sm_i = keep.tile([P, PACK, P, PACK], BF16, name="sm_%d" % i, align_bytes=64)
+            sm_tiles.append(sm_i)
+
+        v_codes = keep.tile([P, HEADS * D], U32, name="v_codes", align_bytes=64)
+        v_scales = keep.tile([P, HEADS * D], U8, name="v_scales", align_bytes=64)
+
+        qk_banks = {}
+        qk_ts = {}
+        decays = {}
+        v_groupeds = {}
+        sm_quantised = {}
+
+        def head_cols(h):
+            return slice((h % GROUP) * D, (h % GROUP + 1) * D)
+
+        def decay_table(h):
+            decay = keep.tile([P, DECAY_COLS], F32, name="decay_%d" % h)
+            nc.scalar.activation(
+                out=decay[:],
+                in_=distance[:],
+                func=EXP,
+                scale=math.log(1.0 - 2.0 ** (-5 - h)),
+                bias=-0.5 * math.log(D),
+            )
+            decays[h] = decay
+
+        def transpose_head(h):
+            qk_ps = psum_t.tile([P, 2 * T], BF16)
+            for c in range(PACK):
+                nc.tensor.transpose(qk_ps[:, c * P : (c + 1) * P], q_sb[h // GROUP][:, c, head_cols(h)], ident[:])
+            for c in range(PACK):
+                nc.tensor.transpose(
+                    qk_ps[:, T + c * P : T + (c + 1) * P], k_sb[h // GROUP][:, c, head_cols(h)], ident[:]
+                )
+            qk_banks[h] = qk_ps
+
+        def copy_transposed(h):
+            qk_t = work.tile([P, 2 * T], BF16)
+            nc.scalar.copy(out=qk_t[:], in_=qk_banks[h][:])
+            qk_ts[h] = qk_t
+
+        def score_set(h, c):
+            qk_t = qk_ts[h]
+            s_ps = psum_s.tile([P, PACK, P], F32, tag="s_ps")
+            for r in range(PACK):
+                slot = PACK - 1 - r
+                nc.tensor.matmul(
+                    out=s_ps[:, r, :],
+                    lhsT=qk_t[:, T + slot * P : T + (slot + 1) * P],
+                    rhs=qk_t[:, c * P : (c + 1) * P],
+                    start=True,
+                    stop=True,
+                )
+            return s_ps
+
+        def decay_of_set(h, c):
+            return decays[h][:, c : c + T].rearrange("p (i r) -> p i r", r=PACK)
+
+        def gpsimd_set(h, c):
+            s_ps = score_set(h, c)
+            s_sb = work.tile([P, P, PACK], F32)
+            nc.scalar.copy(out=s_sb[:], in_=s_ps[:].rearrange("p r i -> p i r"))
+            nc.gpsimd.tensor_tensor(
+                out=sm_tiles[h % SM_BUFS][:, c], in0=s_sb[:], in1=decay_of_set(h, c), op=MULT
+            )
+
+        def vector_set(h, c):
+            s_ps = score_set(h, c)
+            nc.vector.tensor_tensor(
+                out=sm_tiles[h % SM_BUFS][:, c],
+                in0=s_ps[:].rearrange("p r i -> p i r"),
+                in1=decay_of_set(h, c),
+                op=MULT,
+            )
+
+        def quantise_sm(h):
+            sm_codes = work.tile([P, T], U32, align_bytes=64)
+            sm_scales = work.tile([P, T], U8, align_bytes=64)
+            nc.vector.quantize_mx(
+                out=sm_codes[:].bitcast(FP8X4),
+                scales=sm_scales[:],
+                in_=sm_tiles[h % SM_BUFS][:].rearrange("p c i r -> p (c i r)"),
+            )
+            sm_quantised[h] = (sm_codes, sm_scales)
+
+        def regroup_v(g):
+            v_grouped = work.tile([P, V_GROUP_COLS, PACK], BF16, align_bytes=64, bufs=2)
+            nc.vector.tensor_copy(
+                out=v_grouped[:].rearrange("p (e i) r -> p e r i", i=RUN),
+                in_=v_sb[g][:, ::-1, :].rearrange("p r (e i) -> p e r i", i=RUN),
+            )
+            v_groupeds[g] = v_grouped
+
+        def quantise_v(g):
+            cols = slice(g * V_GROUP_COLS, (g + 1) * V_GROUP_COLS)
+            nc.vector.quantize_mx(
+                out=v_codes[:, cols].bitcast(FP8X4),
+                scales=v_scales[:, cols],
+                in_=v_groupeds[g][:].rearrange("p e r -> p (e r)"),
+            )
+
+        def output_head(h):
+            sm_codes, sm_scales = sm_quantised[h]
+            cols = slice(h * D, (h + 1) * D)
+            y_ps = psum_y.tile([P, PACK, D], F32)
+            for c in range(PACK):
+                rows = slice(c * P, (c + 1) * P)
+                nc.tensor.matmul_mx(
+                    out=y_ps[:, c, :],
+                    lhsT=sm_codes[:, rows].bitcast(FP8X4),
+                    lhsT_scale=sm_scales[:, rows],
+                    rhs=v_codes[:, cols].bitcast(FP8X4),
+                    rhs_scale=v_scales[:, cols],
+                    start=True,
+                    stop=True,
+                )
+            y_sb = work.tile([P, PACK, D], F32)
+            nc.scalar.copy(out=y_sb[:], in_=y_ps[:])
+            nc.sync.dma_start(out=out_view[:, :, cols], in_=y_sb[:])
+
+        def is_head(h):
+            return 0 <= h < HEADS
+
+        for h in range(TABLES_AHEAD):
+            decay_table(h)
+        for s in range(-1, HEADS + 3):
+            if is_head(s):
+                copy_transposed(s)
+            if is_head(s - 1):
+                gpsimd_set(s - 1, 0)
+                vector_set(s - 1, 1)
+            if is_head(s - 3):
+                output_head(s - 3)
+            if is_head(s - 2):
+                quantise_sm(s - 2)
+            if is_head(s - 1):
+                vector_set(s - 1, 2)
+                vector_set(s - 1, 3)
+            if is_head(s) and s % V_GROUP == 0:
+                quantise_v(s // V_GROUP)
+            if is_head(s + 1) and (s + 1) % V_GROUP == 0:
+                regroup_v((s + 1) // V_GROUP)
+            if is_head(s + TABLES_AHEAD) and s >= 0:
+                decay_table(s + TABLES_AHEAD)
+            if is_head(s + 1):
+                transpose_head(s + 1)

@@ -219,11 +219,11 @@ def tile_multiscaleretention_pb_kernel(tc, q_rot, k_rot, v, out):
                 vector_set(s - 1, 1)
             if is_head(s - 3):
                 output_head(s - 3)
-            if is_head(s - 2):
-                quantise_sm(s - 2)
             if is_head(s - 1):
                 vector_set(s - 1, 2)
                 vector_set(s - 1, 3)
+            if is_head(s - 2):
+                quantise_sm(s - 2)
             if is_head(s) and s % V_GROUP == 0:
                 quantise_v(s // V_GROUP)
             if is_head(s + 1) and (s + 1) % V_GROUP == 0:

@@ -21,6 +21,7 @@ GROUP = 2
 GROUP_COLS = GROUP * D
 V_GROUP = 4
 V_GROUP_COLS = V_GROUP * D
+V_PAIR = 2
 MASKED = 2.0 ** 30
 RUN = 4
 SM_BUFS = 3
@@ -144,14 +145,6 @@ def tile_multiscaleretention_pb_kernel(tc, q_rot, k_rot, v, out):
         def decay_of_set(h, c):
             return decays[h][:, c : c + T].rearrange("p (i r) -> p i r", r=PACK)
 
-        def gpsimd_set(h, c):
-            s_ps = score_set(h, c)
-            s_sb = work.tile([P, P, PACK], F32)
-            nc.scalar.copy(out=s_sb[:], in_=s_ps[:].rearrange("p r i -> p i r"))
-            nc.gpsimd.tensor_tensor(
-                out=sm_tiles[h % SM_BUFS][:, c], in0=s_sb[:], in1=decay_of_set(h, c), op=MULT
-            )
-
         def vector_set(h, c):
             s_ps = score_set(h, c)
             nc.vector.tensor_tensor(
@@ -171,16 +164,20 @@ def tile_multiscaleretention_pb_kernel(tc, q_rot, k_rot, v, out):
             )
             sm_quantised[h] = (sm_codes, sm_scales)
 
-        def regroup_v(g):
-            v_grouped = work.tile([P, V_GROUP_COLS, PACK], BF16, align_bytes=64, bufs=2)
-            nc.vector.tensor_copy(
-                out=v_grouped[:].rearrange("p (e i) r -> p e r i", i=RUN),
-                in_=v_sb[g][:, ::-1, :].rearrange("p r (e i) -> p e r i", i=RUN),
+        def regroup_v(h):
+            if h % V_PAIR == 0:
+                v_groupeds[h // V_PAIR] = work.tile(
+                    [P, V_PAIR * D, PACK], BF16, name="v_grouped", align_bytes=64, bufs=2
+                )
+            pair_cols = slice((h % V_PAIR) * D, (h % V_PAIR + 1) * D)
+            load_cols = slice((h % V_GROUP) * D, (h % V_GROUP + 1) * D)
+            nc.scalar.copy(
+                out=v_groupeds[h // V_PAIR][:, pair_cols, :].rearrange("p (e i) r -> p e r i", i=RUN),
+                in_=v_sb[h // V_GROUP][:, ::-1, load_cols].rearrange("p r (e i) -> p e r i", i=RUN),
             )
-            v_groupeds[g] = v_grouped
 
         def quantise_v(g):
-            cols = slice(g * V_GROUP_COLS, (g + 1) * V_GROUP_COLS)
+            cols = slice(g * V_PAIR * D, (g + 1) * V_PAIR * D)
             nc.vector.quantize_mx(
                 out=v_codes[:, cols].bitcast(FP8X4),
                 scales=v_scales[:, cols],
@@ -215,19 +212,16 @@ def tile_multiscaleretention_pb_kernel(tc, q_rot, k_rot, v, out):
             if is_head(s):
                 copy_transposed(s)
             if is_head(s - 1):
-                gpsimd_set(s - 1, 0)
-                vector_set(s - 1, 1)
-            if is_head(s - 3):
-                output_head(s - 3)
-            if is_head(s - 1):
-                vector_set(s - 1, 2)
-                vector_set(s - 1, 3)
+                for c in range(PACK):
+                    vector_set(s - 1, c)
             if is_head(s - 2):
                 quantise_sm(s - 2)
-            if is_head(s) and s % V_GROUP == 0:
-                quantise_v(s // V_GROUP)
-            if is_head(s + 1) and (s + 1) % V_GROUP == 0:
-                regroup_v((s + 1) // V_GROUP)
+                if (s - 2) % V_PAIR == 0:
+                    quantise_v((s - 2) // V_PAIR)
+            if is_head(s - 3):
+                output_head(s - 3)
+            if is_head(s):
+                regroup_v(s)
             if is_head(s + TABLES_AHEAD) and s >= 0:
                 decay_table(s + TABLES_AHEAD)
             if is_head(s + 1):

@@ -7,12 +7,15 @@ from concourse.masks import make_identity
 BF16 = mybir.dt.bfloat16
 F32 = mybir.dt.float32
 U32 = mybir.dt.uint32
+I32 = mybir.dt.int32
 U8 = mybir.dt.uint8
 FP8X4 = mybir.dt.float8_e4m3fn_x4
 EXP = mybir.ActivationFunctionType.Exp
 MULT = mybir.AluOpType.mult
+ADD = mybir.AluOpType.add
 
 P = 128
+HALF = P // 2
 PACK = 4
 T = 512
 HEADS = 16
@@ -21,12 +24,15 @@ GROUP = 2
 GROUP_COLS = GROUP * D
 V_GROUP = 4
 V_GROUP_COLS = V_GROUP * D
-V_PAIR = 2
+Y_GROUP = 2
+LOADS_AHEAD = 6
+V_LOADS_AHEAD = 8
 MASKED = 2.0 ** 30
-RUN = 4
 SM_BUFS = 3
+PAD_BUFS = 3
 TABLES_AHEAD = 4
-DECAY_COLS = T + PACK - 1
+LATE_COLS = T // 2 + PACK
+EARLY_COLS = T // 2 + 2
 
 FLOPS = 2 * 2 * HEADS * T * T * D
 
@@ -36,7 +42,7 @@ def tile_multiscaleretention_pb_kernel(tc, q_rot, k_rot, v, out):
     q_view = q_rot.rearrange("b (p c) e -> p (b c) e", c=PACK)
     k_view = k_rot.rearrange("b (p c) e -> p (b c) e", c=PACK)
     v_view = v.rearrange("b (p c) e -> p (b c) e", c=PACK)
-    out_view = out.rearrange("b (p c) e -> p (b c) e", c=PACK)
+    out_view = out.rearrange("b (h i c l) e -> h l i (b c) e", h=2, c=2, l=2)
 
     with ExitStack() as ctx:
         ctx.enter_context(tc.manual_schedule())
@@ -46,64 +52,90 @@ def tile_multiscaleretention_pb_kernel(tc, q_rot, k_rot, v, out):
         psum_s = ctx.enter_context(tc.psum_pool(name="psum_s", bufs=4))
         psum_y = ctx.enter_context(tc.psum_pool(name="psum_y", bufs=2))
 
-        q_sb = []
-        k_sb = []
-        v_sb = []
-        for g in range(HEADS // GROUP):
+        q_sb = {}
+        k_sb = {}
+        v_sb = {}
+
+        def load_qk(g):
             cols = slice(g * GROUP_COLS, (g + 1) * GROUP_COLS)
             q_g = keep.tile([P, PACK, GROUP_COLS], BF16, name="q_g%d" % g)
             k_g = keep.tile([P, PACK, GROUP_COLS], BF16, name="k_g%d" % g)
             nc.sync.dma_start(out=q_g[:], in_=q_view[:, :, cols])
             nc.sync.dma_start(out=k_g[:], in_=k_view[:, :, cols])
-            q_sb.append(q_g)
-            k_sb.append(k_g)
-            if (g * GROUP) % V_GROUP == 0:
-                first = g * GROUP_COLS
-                v_g = keep.tile([P, PACK, V_GROUP_COLS], BF16, name="v_g%d" % len(v_sb))
-                nc.sync.dma_start(out=v_g[:], in_=v_view[:, :, first : first + V_GROUP_COLS])
-                v_sb.append(v_g)
+            q_sb[g] = q_g
+            k_sb[g] = k_g
 
-        distance = keep.tile([P, DECAY_COLS], F32, name="distance")
-        distance_pattern = [[1, DECAY_COLS]]
-        nc.gpsimd.iota(
-            distance[:],
-            pattern=distance_pattern,
-            base=1 - PACK,
-            channel_multiplier=-PACK,
-            allow_small_or_imprecise_dtypes=True,
-        )
-        nc.gpsimd.affine_select(
-            out=distance[:],
-            in_=distance[:],
-            pattern=distance_pattern,
-            compare_op=mybir.AluOpType.is_ge,
-            fill=MASKED,
-            base=1 - PACK,
-            channel_multiplier=-PACK,
-        )
+        def load_v(g):
+            cols = slice(g * V_GROUP_COLS, (g + 1) * V_GROUP_COLS)
+            v_g = keep.tile([P, PACK, V_GROUP_COLS], BF16, name="v_g%d" % g)
+            nc.sync.dma_start(out=v_g[:], in_=v_view[:, :, cols])
+            v_sb[g] = v_g
+
+        load_qk(0)
+        load_v(0)
+        load_qk(1)
+        load_v(1)
+        load_qk(2)
 
         ident = keep.tile([P, P], BF16, name="ident")
         make_identity(nc, ident[:])
+        distance = keep.tile([P, LATE_COLS + EARLY_COLS], F32, name="distance")
+
+        def fill_distance(part, width, base):
+            pattern = [[1, width]]
+            nc.gpsimd.iota(
+                part, pattern=pattern, base=base, channel_multiplier=-PACK, allow_small_or_imprecise_dtypes=True
+            )
+            nc.gpsimd.affine_select(
+                out=part,
+                in_=part,
+                pattern=pattern,
+                compare_op=mybir.AluOpType.is_ge,
+                fill=MASKED,
+                base=base,
+                channel_multiplier=-PACK,
+            )
+
+        fill_distance(distance[:, 0:LATE_COLS], LATE_COLS, T // 2 - 3)
+        fill_distance(distance[0:HALF, LATE_COLS:], EARLY_COLS, -3)
+        fill_distance(distance[HALF:P, LATE_COLS:], EARLY_COLS, -1)
+
+        k_pads = []
+        for i in range(PAD_BUFS):
+            k_pad = keep.tile([P, PACK, 3 * HALF], BF16, name="k_pad_%d" % i)
+            nc.vector.memset(k_pad[:].bitcast(U32), 0)
+            k_pads.append(k_pad)
 
         sm_tiles = []
         for i in range(SM_BUFS):
-            sm_i = keep.tile([P, PACK, P, PACK], BF16, name="sm_%d" % i, align_bytes=64)
+            sm_i = keep.tile([P, 3, P, PACK], BF16, name="sm_%d" % i, align_bytes=64)
             sm_tiles.append(sm_i)
 
         v_codes = keep.tile([P, HEADS * D], U32, name="v_codes", align_bytes=64)
         v_scales = keep.tile([P, HEADS * D], U8, name="v_scales", align_bytes=64)
+        nc.vector.memset(v_scales[:].bitcast(U32), 0)
+        v_pair_codes = []
+        v_pair_scales = []
+        for g in range(HEADS // V_GROUP):
+            codes_g = keep.tile([P, V_GROUP, 2, D], U32, name="v_pair_codes_%d" % g, align_bytes=64)
+            scales_g = keep.tile([P, V_GROUP, 2, D], U8, name="v_pair_scales_%d" % g, align_bytes=64)
+            nc.vector.memset(codes_g[:], 0)
+            nc.vector.memset(scales_g[:].bitcast(U32), 0)
+            v_pair_codes.append(codes_g)
+            v_pair_scales.append(scales_g)
 
         qk_banks = {}
         qk_ts = {}
         decays = {}
         v_groupeds = {}
         sm_quantised = {}
+        y_sbs = {}
 
         def head_cols(h):
             return slice((h % GROUP) * D, (h % GROUP + 1) * D)
 
         def decay_table(h):
-            decay = keep.tile([P, DECAY_COLS], F32, name="decay_%d" % h)
+            decay = keep.tile([P, LATE_COLS + EARLY_COLS], F32, name="decay_%d" % h)
             nc.scalar.activation(
                 out=decay[:],
                 in_=distance[:],
@@ -114,84 +146,111 @@ def tile_multiscaleretention_pb_kernel(tc, q_rot, k_rot, v, out):
             decays[h] = decay
 
         def transpose_head(h):
-            qk_ps = psum_t.tile([P, 2 * T], BF16)
+            qk_ps = psum_t.tile([P, 2 * PACK, P], BF16)
             for c in range(PACK):
-                nc.tensor.transpose(qk_ps[:, c * P : (c + 1) * P], q_sb[h // GROUP][:, c, head_cols(h)], ident[:])
+                nc.tensor.transpose(qk_ps[:, c, :], q_sb[h // GROUP][:, c, head_cols(h)], ident[:])
             for c in range(PACK):
-                nc.tensor.transpose(
-                    qk_ps[:, T + c * P : T + (c + 1) * P], k_sb[h // GROUP][:, c, head_cols(h)], ident[:]
-                )
+                nc.tensor.transpose(qk_ps[:, PACK + c, :], k_sb[h // GROUP][:, c, head_cols(h)], ident[:])
             qk_banks[h] = qk_ps
 
         def copy_transposed(h):
-            qk_t = work.tile([P, 2 * T], BF16)
+            qk_t = work.tile([P, 2 * PACK, P], BF16)
             nc.scalar.copy(out=qk_t[:], in_=qk_banks[h][:])
+            nc.scalar.copy(out=k_pads[h % PAD_BUFS][:, :, HALF:P], in_=qk_banks[h][:, PACK:, 0:HALF])
             qk_ts[h] = qk_t
 
-        def score_set(h, c):
+        def late_bank(h, b):
             qk_t = qk_ts[h]
-            s_ps = psum_s.tile([P, PACK, P], F32, tag="s_ps")
+            s_ps = psum_s.tile([P, PACK, 2, HALF], F32, tag="s_ps")
             for r in range(PACK):
-                slot = PACK - 1 - r
                 nc.tensor.matmul(
-                    out=s_ps[:, r, :],
-                    lhsT=qk_t[:, T + slot * P : T + (slot + 1) * P],
-                    rhs=qk_t[:, c * P : (c + 1) * P],
+                    out=s_ps[:, r],
+                    lhsT=qk_t[:, 2 * PACK - 1 - r, :],
+                    rhs=qk_t[:, 2 * b : 2 * b + 2, HALF:P],
                     start=True,
                     stop=True,
                 )
-            return s_ps
+            for l in range(2):
+                decay_set(h, s_ps, b, l, 2 * b + l)
 
-        def decay_of_set(h, c):
-            return decays[h][:, c : c + T].rearrange("p (i r) -> p i r", r=PACK)
+        def early_bank(h):
+            qk_t = qk_ts[h]
+            k_pad = k_pads[h % PAD_BUFS]
+            s_ps = psum_s.tile([P, PACK, 2, HALF], F32, tag="s_ps")
+            for r in range(PACK):
+                slot = PACK - 1 - r
+                nc.tensor.matmul(
+                    out=s_ps[:, r], lhsT=k_pad[:, slot, HALF:], rhs=qk_t[:, 0:2, 0:HALF], start=True, stop=False
+                )
+                nc.tensor.matmul(
+                    out=s_ps[:, r], lhsT=k_pad[:, slot, 0:P], rhs=qk_t[:, 2:4, 0:HALF], start=False, stop=True
+                )
+            for l in range(2):
+                decay_set(h, s_ps, 2, l, LATE_COLS + l)
 
-        def vector_set(h, c):
-            s_ps = score_set(h, c)
+        def decay_set(h, s_ps, b, l, first):
             nc.vector.tensor_tensor(
-                out=sm_tiles[h % SM_BUFS][:, c],
-                in0=s_ps[:].rearrange("p r i -> p i r"),
-                in1=decay_of_set(h, c),
+                out=sm_tiles[h % SM_BUFS][:, b, l * HALF : (l + 1) * HALF, :],
+                in0=s_ps[:, :, l, :].rearrange("p r i -> p i r"),
+                in1=decays[h][:, first : first + T // 2].rearrange("p (i r) -> p i r", r=PACK),
                 op=MULT,
             )
 
         def quantise_sm(h):
-            sm_codes = work.tile([P, T], U32, align_bytes=64)
-            sm_scales = work.tile([P, T], U8, align_bytes=64)
-            nc.vector.quantize_mx(
-                out=sm_codes[:].bitcast(FP8X4),
-                scales=sm_scales[:],
-                in_=sm_tiles[h % SM_BUFS][:].rearrange("p c i r -> p (c i r)"),
-            )
+            sm_codes = work.tile([P, 3 * P], U32, align_bytes=64)
+            sm_scales = work.tile([P, 3 * P], U8, align_bytes=64)
+            for first, last in ((0, 2), (2, 3)):
+                cols = slice(first * P, last * P)
+                nc.vector.quantize_mx(
+                    out=sm_codes[:, cols].bitcast(FP8X4),
+                    scales=sm_scales[:, cols],
+                    in_=sm_tiles[h % SM_BUFS][:, first:last].rearrange("p b m r -> p (b m r)"),
+                )
             sm_quantised[h] = (sm_codes, sm_scales)
 
         def regroup_v(h):
-            if h % V_PAIR == 0:
-                v_groupeds[h // V_PAIR] = work.tile(
-                    [P, V_PAIR * D, PACK], BF16, name="v_grouped", align_bytes=64, bufs=2
-                )
-            pair_cols = slice((h % V_PAIR) * D, (h % V_PAIR + 1) * D)
-            load_cols = slice((h % V_GROUP) * D, (h % V_GROUP + 1) * D)
-            nc.scalar.copy(
-                out=v_groupeds[h // V_PAIR][:, pair_cols, :].rearrange("p (e i) r -> p e r i", i=RUN),
-                in_=v_sb[h // V_GROUP][:, ::-1, load_cols].rearrange("p r (e i) -> p e r i", i=RUN),
+            g = h // V_GROUP
+            if h % V_GROUP == 0:
+                v_groupeds[g] = work.tile([P, V_GROUP_COLS, PACK], BF16, name="v_grouped", align_bytes=64, bufs=2)
+            cols = slice((h % V_GROUP) * D, (h % V_GROUP + 1) * D)
+            nc.gpsimd.tensor_scalar(
+                out=v_groupeds[g][:, cols, :],
+                in0=v_sb[g][:, ::-1, cols].rearrange("p r e -> p e r"),
+                scalar1=1.0,
+                scalar2=0.0,
+                op0=MULT,
+                op1=ADD,
             )
 
         def quantise_v(g):
-            cols = slice(g * V_PAIR * D, (g + 1) * V_PAIR * D)
+            cols = slice(g * V_GROUP_COLS, (g + 1) * V_GROUP_COLS)
             nc.vector.quantize_mx(
                 out=v_codes[:, cols].bitcast(FP8X4),
                 scales=v_scales[:, cols],
                 in_=v_groupeds[g][:].rearrange("p e r -> p (e r)"),
             )
+            for half in range(2):
+                rows = slice(half * HALF, (half + 1) * HALF)
+                nc.sync.dma_start(
+                    out=v_pair_codes[g][rows, :, half, :].bitcast(I32),
+                    in_=v_codes[0:HALF, cols].bitcast(I32).rearrange("p (h e) -> p h e", h=V_GROUP),
+                )
+                nc.sync.dma_start(
+                    out=v_pair_scales[g][rows, :, half, :].bitcast(I32),
+                    in_=v_scales[0:HALF, cols].bitcast(I32).rearrange("p (h e) -> p h e", h=V_GROUP),
+                )
 
         def output_head(h):
             sm_codes, sm_scales = sm_quantised[h]
             cols = slice(h * D, (h + 1) * D)
-            y_ps = psum_y.tile([P, PACK, D], F32)
-            for c in range(PACK):
-                rows = slice(c * P, (c + 1) * P)
+            g = h // V_GROUP
+            pair_codes = v_pair_codes[g][:, h % V_GROUP].rearrange("p a e -> p (a e)")
+            pair_scales = v_pair_scales[g][:, h % V_GROUP].rearrange("p a e -> p (a e)")
+            y_ps = psum_y.tile([P, 2, 2, D], F32)
+            for b in range(2):
+                rows = slice(b * P, (b + 1) * P)
                 nc.tensor.matmul_mx(
-                    out=y_ps[:, c, :],
+                    out=y_ps[:, 1, b, :],
                     lhsT=sm_codes[:, rows].bitcast(FP8X4),
                     lhsT_scale=sm_scales[:, rows],
                     rhs=v_codes[:, cols].bitcast(FP8X4),
@@ -199,30 +258,58 @@ def tile_multiscaleretention_pb_kernel(tc, q_rot, k_rot, v, out):
                     start=True,
                     stop=True,
                 )
-            y_sb = work.tile([P, PACK, D], F32)
-            nc.scalar.copy(out=y_sb[:], in_=y_ps[:])
-            nc.sync.dma_start(out=out_view[:, :, cols], in_=y_sb[:])
+            rows = slice(2 * P, 3 * P)
+            nc.tensor.matmul_mx(
+                out=y_ps[:, 0].rearrange("p c e -> p (c e)"),
+                lhsT=sm_codes[:, rows].bitcast(FP8X4),
+                lhsT_scale=sm_scales[:, rows],
+                rhs=pair_codes.bitcast(FP8X4),
+                rhs_scale=pair_scales,
+                start=True,
+                stop=True,
+            )
+            gy = h // Y_GROUP
+            if h % Y_GROUP == 0:
+                y_sbs[gy] = work.tile([P, 2, 2, Y_GROUP * D], F32, name="y_sb")
+            y_sb = y_sbs[gy]
+            nc.scalar.copy(out=y_sb[:, :, :, (h % Y_GROUP) * D : (h % Y_GROUP + 1) * D], in_=y_ps[:])
+            if h % Y_GROUP == Y_GROUP - 1:
+                out_cols = slice(gy * Y_GROUP * D, (gy + 1) * Y_GROUP * D)
+                for half in range(2):
+                    for l in range(2):
+                        nc.sync.dma_start(
+                            out=out_view[half, l][:, :, out_cols], in_=y_sb[l * HALF : (l + 1) * HALF, half]
+                        )
 
         def is_head(h):
             return 0 <= h < HEADS
 
-        for h in range(TABLES_AHEAD):
-            decay_table(h)
+        for h in range(V_GROUP):
+            regroup_v(h)
         for s in range(-1, HEADS + 3):
+            if is_head(s + LOADS_AHEAD) and s >= 0 and (s + LOADS_AHEAD) % GROUP == 0:
+                load_qk((s + LOADS_AHEAD) // GROUP)
+            if is_head(s + V_LOADS_AHEAD) and s >= 0 and s % V_GROUP == 0:
+                load_v((s + V_LOADS_AHEAD) // V_GROUP)
             if is_head(s):
                 copy_transposed(s)
             if is_head(s - 1):
-                for c in range(PACK):
-                    vector_set(s - 1, c)
+                late_bank(s - 1, 0)
+                late_bank(s - 1, 1)
+                early_bank(s - 1)
             if is_head(s - 2):
                 quantise_sm(s - 2)
-                if (s - 2) % V_PAIR == 0:
-                    quantise_v((s - 2) // V_PAIR)
+            if is_head(s - 1) and (s - 1) % V_GROUP == 0:
+                quantise_v((s - 1) // V_GROUP)
             if is_head(s - 3):
                 output_head(s - 3)
+            if s >= 1 and is_head(s - 1 + V_GROUP):
+                regroup_v(s - 1 + V_GROUP)
             if is_head(s):
-                regroup_v(s)
-            if is_head(s + TABLES_AHEAD) and s >= 0:
-                decay_table(s + TABLES_AHEAD)
+                for h in range(s * 2, s * 2 + 2):
+                    if is_head(h) and h < TABLES_AHEAD * 2:
+                        decay_table(h)
+                if s >= TABLES_AHEAD and is_head(s + TABLES_AHEAD):
+                    decay_table(s + TABLES_AHEAD)
             if is_head(s + 1):
                 transpose_head(s + 1)

@@ -28,6 +28,7 @@ Y_GROUP = 2
 LOADS_AHEAD = 6
 V_LOADS_AHEAD = 8
 MASKED = 2.0 ** 30
+SM_RUN = 2
 SM_BUFS = 3
 PAD_BUFS = 3
 TABLES_AHEAD = 4
@@ -189,10 +190,11 @@ def tile_multiscaleretention_pb_kernel(tc, q_rot, k_rot, v, out):
                 decay_set(h, s_ps, 2, l, LATE_COLS + l)
 
         def decay_set(h, s_ps, b, l, first):
+            sm_part = sm_tiles[h % SM_BUFS][:, b, l * HALF : (l + 1) * HALF, :]
             nc.vector.tensor_tensor(
-                out=sm_tiles[h % SM_BUFS][:, b, l * HALF : (l + 1) * HALF, :],
-                in0=s_ps[:, :, l, :].rearrange("p r i -> p i r"),
-                in1=decays[h][:, first : first + T // 2].rearrange("p (i r) -> p i r", r=PACK),
+                out=sm_part.rearrange("p (i a) r -> p i r a", a=SM_RUN),
+                in0=s_ps[:, :, l, :].rearrange("p r (i a) -> p i r a", a=SM_RUN),
+                in1=decays[h][:, first : first + T // 2].rearrange("p (i a r) -> p i r a", a=SM_RUN, r=PACK),
                 op=MULT,
             )
 

@@ -12,7 +12,6 @@ U8 = mybir.dt.uint8
 FP8X4 = mybir.dt.float8_e4m3fn_x4
 EXP = mybir.ActivationFunctionType.Exp
 MULT = mybir.AluOpType.mult
-ADD = mybir.AluOpType.add
 
 P = 128
 HALF = P // 2
@@ -28,6 +27,7 @@ Y_GROUP = 2
 LOADS_AHEAD = 6
 V_LOADS_AHEAD = 8
 MASKED = 2.0 ** 30
+V_RUN = 4
 SM_RUN = 2
 SM_BUFS = 3
 PAD_BUFS = 3
@@ -215,13 +215,9 @@ def tile_multiscaleretention_pb_kernel(tc, q_rot, k_rot, v, out):
             if h % V_GROUP == 0:
                 v_groupeds[g] = work.tile([P, V_GROUP_COLS, PACK], BF16, name="v_grouped", align_bytes=64, bufs=2)
             cols = slice((h % V_GROUP) * D, (h % V_GROUP + 1) * D)
-            nc.gpsimd.tensor_scalar(
-                out=v_groupeds[g][:, cols, :],
-                in0=v_sb[g][:, ::-1, cols].rearrange("p r e -> p e r"),
-                scalar1=1.0,
-                scalar2=0.0,
-                op0=MULT,
-                op1=ADD,
+            nc.scalar.copy(
+                out=v_groupeds[g][:, cols, :].rearrange("p (e i) r -> p e r i", i=V_RUN),
+                in_=v_sb[g][:, ::-1, cols].rearrange("p r (e i) -> p e r i", i=V_RUN),
             )
 
         def quantise_v(g):
@@ -286,8 +282,6 @@ def tile_multiscaleretention_pb_kernel(tc, q_rot, k_rot, v, out):
         def is_head(h):
             return 0 <= h < HEADS
 
-        for h in range(V_GROUP):
-            regroup_v(h)
         for s in range(-1, HEADS + 3):
             if is_head(s + LOADS_AHEAD) and s >= 0 and (s + LOADS_AHEAD) % GROUP == 0:
                 load_qk((s + LOADS_AHEAD) // GROUP)
@@ -295,6 +289,9 @@ def tile_multiscaleretention_pb_kernel(tc, q_rot, k_rot, v, out):
                 load_v((s + V_LOADS_AHEAD) // V_GROUP)
             if is_head(s):
                 copy_transposed(s)
+            if s == 0:
+                for h in range(V_GROUP):
+                    regroup_v(h)
             if is_head(s - 1):
                 late_bank(s - 1, 0)
                 late_bank(s - 1, 1)

@@ -156,8 +156,10 @@ def tile_multiscaleretention_pb_kernel(tc, q_rot, k_rot, v, out):
 
         def copy_transposed(h):
             qk_t = work.tile([P, 2 * PACK, P], BF16)
-            nc.scalar.copy(out=qk_t[:], in_=qk_banks[h][:])
-            nc.scalar.copy(out=k_pads[h % PAD_BUFS][:, :, HALF:P], in_=qk_banks[h][:, PACK:, 0:HALF])
+            nc.scalar.copy(out=qk_t[:].bitcast(F32), in_=qk_banks[h][:].bitcast(F32))
+            nc.scalar.copy(
+                out=k_pads[h % PAD_BUFS][:, :, HALF:P].bitcast(F32), in_=qk_banks[h][:, PACK:, 0:HALF].bitcast(F32)
+            )
             qk_ts[h] = qk_t
 
         def late_bank(h, b):

@@ -19,21 +19,17 @@ PACK = 4
 T = 512
 HEADS = 16
 D = 128
-GROUP = 2
-GROUP_COLS = GROUP * D
 V_GROUP = 4
 V_GROUP_COLS = V_GROUP * D
-Y_GROUP = 2
-LOADS_AHEAD = 6
-V_LOADS_AHEAD = 8
+STORES = ((0, 4), (4, 8), (8, 12), (12, 14), (14, 15), (15, 16))
+STORE_COLS = 4 * D
 MASKED = 2.0 ** 30
 V_RUN = 4
-SM_RUN = 2
+SM_BLOCKS = 3
 SM_BUFS = 3
 PAD_BUFS = 3
 TABLES_AHEAD = 4
-LATE_COLS = T // 2 + PACK
-EARLY_COLS = T // 2 + 2
+DECAY_COLS = T // 2 + PACK
 
 FLOPS = 2 * 2 * HEADS * T * T * D
 
@@ -57,33 +53,32 @@ def tile_multiscaleretention_pb_kernel(tc, q_rot, k_rot, v, out):
         k_sb = {}
         v_sb = {}
 
-        def load_qk(g):
-            cols = slice(g * GROUP_COLS, (g + 1) * GROUP_COLS)
-            q_g = keep.tile([P, PACK, GROUP_COLS], BF16, name="q_g%d" % g)
-            k_g = keep.tile([P, PACK, GROUP_COLS], BF16, name="k_g%d" % g)
-            nc.sync.dma_start(out=q_g[:], in_=q_view[:, :, cols])
-            nc.sync.dma_start(out=k_g[:], in_=k_view[:, :, cols])
-            q_sb[g] = q_g
-            k_sb[g] = k_g
+        def load(source, view, tiles, first, last):
+            tile = keep.tile([P, PACK, (last - first) * D], BF16, name="%s_%d" % (source, first))
+            nc.sync.dma_start(out=tile[:], in_=view[:, :, first * D : last * D])
+            for h in range(first, last):
+                tiles[h] = tile[:, :, (h - first) * D : (h - first + 1) * D]
+            return tile
 
-        def load_v(g):
-            cols = slice(g * V_GROUP_COLS, (g + 1) * V_GROUP_COLS)
-            v_g = keep.tile([P, PACK, V_GROUP_COLS], BF16, name="v_g%d" % g)
-            nc.sync.dma_start(out=v_g[:], in_=v_view[:, :, cols])
-            v_sb[g] = v_g
+        def load_qk(first, last):
+            load("q", q_view, q_sb, first, last)
+            load("k", k_view, k_sb, first, last)
 
-        load_qk(0)
-        load_v(0)
-        load_qk(1)
-        load_v(1)
-        load_qk(2)
+        def load_v(first, last):
+            return load("v", v_view, v_sb, first, last)
+
+        load_qk(0, 2)
+        v_first = load_v(0, 4)
+        load_qk(2, 4)
+        load_v(4, 8)
+        load_qk(4, 8)
 
         ident = keep.tile([P, P], BF16, name="ident")
         make_identity(nc, ident[:])
-        distance = keep.tile([P, LATE_COLS + EARLY_COLS], F32, name="distance")
+        distance = keep.tile([P, 2, DECAY_COLS], F32, name="distance")
 
-        def fill_distance(part, width, base):
-            pattern = [[1, width]]
+        def fill_distance(part, base):
+            pattern = [[1, DECAY_COLS]]
             nc.gpsimd.iota(
                 part, pattern=pattern, base=base, channel_multiplier=-PACK, allow_small_or_imprecise_dtypes=True
             )
@@ -97,9 +92,9 @@ def tile_multiscaleretention_pb_kernel(tc, q_rot, k_rot, v, out):
                 channel_multiplier=-PACK,
             )
 
-        fill_distance(distance[:, 0:LATE_COLS], LATE_COLS, T // 2 - 3)
-        fill_distance(distance[0:HALF, LATE_COLS:], EARLY_COLS, -3)
-        fill_distance(distance[HALF:P, LATE_COLS:], EARLY_COLS, -1)
+        fill_distance(distance[:, 0], T // 2 - 3)
+        fill_distance(distance[0:HALF, 1], -3)
+        fill_distance(distance[HALF:P, 1], -1)
 
         k_pads = []
         for i in range(PAD_BUFS):
@@ -109,7 +104,7 @@ def tile_multiscaleretention_pb_kernel(tc, q_rot, k_rot, v, out):
 
         sm_tiles = []
         for i in range(SM_BUFS):
-            sm_i = keep.tile([P, 3, P, PACK], BF16, name="sm_%d" % i, align_bytes=64)
+            sm_i = keep.tile([P, 2, SM_BLOCKS, P, PACK], BF16, name="sm_%d" % i, align_bytes=64)
             sm_tiles.append(sm_i)
 
         v_codes = keep.tile([P, HEADS * D], U32, name="v_codes", align_bytes=64)
@@ -120,8 +115,9 @@ def tile_multiscaleretention_pb_kernel(tc, q_rot, k_rot, v, out):
         for g in range(HEADS // V_GROUP):
             codes_g = keep.tile([P, V_GROUP, 2, D], U32, name="v_pair_codes_%d" % g, align_bytes=64)
             scales_g = keep.tile([P, V_GROUP, 2, D], U8, name="v_pair_scales_%d" % g, align_bytes=64)
-            nc.vector.memset(codes_g[:], 0)
-            nc.vector.memset(scales_g[:].bitcast(U32), 0)
+            zeroing = nc.vector if g < 2 else nc.gpsimd
+            zeroing.memset(codes_g[:], 0)
+            zeroing.memset(scales_g[:].bitcast(U32), 0)
             v_pair_codes.append(codes_g)
             v_pair_scales.append(scales_g)
 
@@ -132,11 +128,8 @@ def tile_multiscaleretention_pb_kernel(tc, q_rot, k_rot, v, out):
         sm_quantised = {}
         y_sbs = {}
 
-        def head_cols(h):
-            return slice((h % GROUP) * D, (h % GROUP + 1) * D)
-
         def decay_table(h):
-            decay = keep.tile([P, LATE_COLS + EARLY_COLS], F32, name="decay_%d" % h)
+            decay = keep.tile([P, 2, DECAY_COLS], F32, name="decay_%d" % h)
             nc.scalar.activation(
                 out=decay[:],
                 in_=distance[:],
@@ -149,9 +142,9 @@ def tile_multiscaleretention_pb_kernel(tc, q_rot, k_rot, v, out):
         def transpose_head(h):
             qk_ps = psum_t.tile([P, 2 * PACK, P], BF16)
             for c in range(PACK):
-                nc.tensor.transpose(qk_ps[:, c, :], q_sb[h // GROUP][:, c, head_cols(h)], ident[:])
+                nc.tensor.transpose(qk_ps[:, c, :], q_sb[h][:, c, :], ident[:])
             for c in range(PACK):
-                nc.tensor.transpose(qk_ps[:, PACK + c, :], k_sb[h // GROUP][:, c, head_cols(h)], ident[:])
+                nc.tensor.transpose(qk_ps[:, PACK + c, :], k_sb[h][:, c, :], ident[:])
             qk_banks[h] = qk_ps
 
         def copy_transposed(h):
@@ -162,64 +155,69 @@ def tile_multiscaleretention_pb_kernel(tc, q_rot, k_rot, v, out):
             )
             qk_ts[h] = qk_t
 
-        def late_bank(h, b):
-            qk_t = qk_ts[h]
-            s_ps = psum_s.tile([P, PACK, 2, HALF], F32, tag="s_ps")
-            for r in range(PACK):
-                nc.tensor.matmul(
-                    out=s_ps[:, r],
-                    lhsT=qk_t[:, 2 * PACK - 1 - r, :],
-                    rhs=qk_t[:, 2 * b : 2 * b + 2, HALF:P],
-                    start=True,
-                    stop=True,
-                )
-            for l in range(2):
-                decay_set(h, s_ps, b, l, 2 * b + l)
+        def key_slot(h, r):
+            return qk_ts[h][:, 2 * PACK - 1 - r, :]
 
-        def early_bank(h):
+        def mixed_bank(h, l):
             qk_t = qk_ts[h]
             k_pad = k_pads[h % PAD_BUFS]
             s_ps = psum_s.tile([P, PACK, 2, HALF], F32, tag="s_ps")
             for r in range(PACK):
                 slot = PACK - 1 - r
                 nc.tensor.matmul(
-                    out=s_ps[:, r], lhsT=k_pad[:, slot, HALF:], rhs=qk_t[:, 0:2, 0:HALF], start=True, stop=False
+                    out=s_ps[:, r, 0], lhsT=key_slot(h, r), rhs=qk_t[:, l, HALF:P], start=True, stop=True
                 )
                 nc.tensor.matmul(
-                    out=s_ps[:, r], lhsT=k_pad[:, slot, 0:P], rhs=qk_t[:, 2:4, 0:HALF], start=False, stop=True
+                    out=s_ps[:, r, 1], lhsT=k_pad[:, slot, HALF:], rhs=qk_t[:, l, 0:HALF], start=True, stop=False
                 )
-            for l in range(2):
-                decay_set(h, s_ps, 2, l, LATE_COLS + l)
-
-        def decay_set(h, s_ps, b, l, first):
-            sm_part = sm_tiles[h % SM_BUFS][:, b, l * HALF : (l + 1) * HALF, :]
+                nc.tensor.matmul(
+                    out=s_ps[:, r, 1], lhsT=k_pad[:, slot, 0:P], rhs=qk_t[:, l + 2, 0:HALF], start=False, stop=True
+                )
             nc.vector.tensor_tensor(
-                out=sm_part.rearrange("p (i a) r -> p i r a", a=SM_RUN),
-                in0=s_ps[:, :, l, :].rearrange("p r (i a) -> p i r a", a=SM_RUN),
-                in1=decays[h][:, first : first + T // 2].rearrange("p (i a r) -> p i r a", a=SM_RUN, r=PACK),
+                out=sm_tiles[h // 2 % SM_BUFS][:, h % 2, 0:3:2, l * HALF : (l + 1) * HALF, :],
+                in0=s_ps[:].rearrange("p r b i -> p b i r"),
+                in1=decays[h][:, :, l : l + T // 2].rearrange("p b (i r) -> p b i r", r=PACK),
                 op=MULT,
             )
 
-        def quantise_sm(h):
-            sm_codes = work.tile([P, 3 * P], U32, align_bytes=64)
-            sm_scales = work.tile([P, 3 * P], U8, align_bytes=64)
-            for first, last in ((0, 2), (2, 3)):
-                cols = slice(first * P, last * P)
-                nc.vector.quantize_mx(
-                    out=sm_codes[:, cols].bitcast(FP8X4),
-                    scales=sm_scales[:, cols],
-                    in_=sm_tiles[h % SM_BUFS][:, first:last].rearrange("p b m r -> p (b m r)"),
+        def late_bank(h):
+            qk_t = qk_ts[h]
+            s_ps = psum_s.tile([P, PACK, 2, HALF], F32, tag="s_ps")
+            for r in range(PACK):
+                nc.tensor.matmul(
+                    out=s_ps[:, r], lhsT=key_slot(h, r), rhs=qk_t[:, 2:4, HALF:P], start=True, stop=True
                 )
-            sm_quantised[h] = (sm_codes, sm_scales)
+            for l in range(2):
+                nc.vector.tensor_tensor(
+                    out=sm_tiles[h // 2 % SM_BUFS][:, h % 2, 1, l * HALF : (l + 1) * HALF, :],
+                    in0=s_ps[:, :, l, :].rearrange("p r i -> p i r"),
+                    in1=decays[h][:, 0, 2 + l : 2 + l + T // 2].rearrange("p (i r) -> p i r", r=PACK),
+                    op=MULT,
+                )
 
-        def regroup_v(h):
+        def quantise_sm(pair, first, last):
+            if first == 0:
+                sm_codes = work.tile([P, 2 * SM_BLOCKS * P], U32, align_bytes=64)
+                sm_scales = work.tile([P, 2 * SM_BLOCKS * P], U8, align_bytes=64)
+                sm_quantised[pair] = (sm_codes, sm_scales)
+            sm_codes, sm_scales = sm_quantised[pair]
+            cols = slice(first * P, last * P)
+            nc.vector.quantize_mx(
+                out=sm_codes[:, cols].bitcast(FP8X4),
+                scales=sm_scales[:, cols],
+                in_=sm_tiles[pair % SM_BUFS][:].rearrange("p h b m r -> p (h b m r)")[
+                    :, first * P * PACK : last * P * PACK
+                ],
+            )
+
+        def regroup_v(copy, h, source):
             g = h // V_GROUP
             if h % V_GROUP == 0:
                 v_groupeds[g] = work.tile([P, V_GROUP_COLS, PACK], BF16, name="v_grouped", align_bytes=64, bufs=2)
-            cols = slice((h % V_GROUP) * D, (h % V_GROUP + 1) * D)
-            nc.scalar.copy(
+            cols = slice((h % V_GROUP) * D, (h % V_GROUP) * D + source.shape[2])
+            copy(
                 out=v_groupeds[g][:, cols, :].rearrange("p (e i) r -> p e r i", i=V_RUN),
-                in_=v_sb[g][:, ::-1, cols].rearrange("p r (e i) -> p e r i", i=V_RUN),
+                in_=source[:, ::-1, :].rearrange("p r (e i) -> p e r i", i=V_RUN),
             )
 
         def quantise_v(g):
@@ -229,6 +227,9 @@ def tile_multiscaleretention_pb_kernel(tc, q_rot, k_rot, v, out):
                 scales=v_scales[:, cols],
                 in_=v_groupeds[g][:].rearrange("p e r -> p (e r)"),
             )
+
+        def pair_v(g):
+            cols = slice(g * V_GROUP_COLS, (g + 1) * V_GROUP_COLS)
             for half in range(2):
                 rows = slice(half * HALF, (half + 1) * HALF)
                 nc.sync.dma_start(
@@ -241,14 +242,15 @@ def tile_multiscaleretention_pb_kernel(tc, q_rot, k_rot, v, out):
                 )
 
         def output_head(h):
-            sm_codes, sm_scales = sm_quantised[h]
+            sm_codes, sm_scales = sm_quantised[h // 2]
+            block = (h % 2) * SM_BLOCKS
             cols = slice(h * D, (h + 1) * D)
             g = h // V_GROUP
             pair_codes = v_pair_codes[g][:, h % V_GROUP].rearrange("p a e -> p (a e)")
             pair_scales = v_pair_scales[g][:, h % V_GROUP].rearrange("p a e -> p (a e)")
             y_ps = psum_y.tile([P, 2, 2, D], F32)
             for b in range(2):
-                rows = slice(b * P, (b + 1) * P)
+                rows = slice((block + b) * P, (block + b + 1) * P)
                 nc.tensor.matmul_mx(
                     out=y_ps[:, 1, b, :],
                     lhsT=sm_codes[:, rows].bitcast(FP8X4),
@@ -258,7 +260,7 @@ def tile_multiscaleretention_pb_kernel(tc, q_rot, k_rot, v, out):
                     start=True,
                     stop=True,
                 )
-            rows = slice(2 * P, 3 * P)
+            rows = slice((block + 2) * P, (block + 3) * P)
             nc.tensor.matmul_mx(
                 out=y_ps[:, 0].rearrange("p c e -> p (c e)"),
                 lhsT=sm_codes[:, rows].bitcast(FP8X4),
@@ -268,44 +270,44 @@ def tile_multiscaleretention_pb_kernel(tc, q_rot, k_rot, v, out):
                 start=True,
                 stop=True,
             )
-            gy = h // Y_GROUP
-            if h % Y_GROUP == 0:
-                y_sbs[gy] = work.tile([P, 2, 2, Y_GROUP * D], F32, name="y_sb")
-            y_sb = y_sbs[gy]
-            nc.scalar.copy(out=y_sb[:, :, :, (h % Y_GROUP) * D : (h % Y_GROUP + 1) * D], in_=y_ps[:])
-            if h % Y_GROUP == Y_GROUP - 1:
-                out_cols = slice(gy * Y_GROUP * D, (gy + 1) * Y_GROUP * D)
+            first, last = [store for store in STORES if store[0] <= h < store[1]][0]
+            if h == first:
+                y_sbs[first] = work.tile([P, 2, 2, STORE_COLS], F32, name="y_sb")
+            y_sb = y_sbs[first]
+            nc.scalar.copy(out=y_sb[:, :, :, (h - first) * D : (h - first + 1) * D], in_=y_ps[:])
+            if h == last - 1:
                 for half in range(2):
                     for l in range(2):
                         nc.sync.dma_start(
-                            out=out_view[half, l][:, :, out_cols], in_=y_sb[l * HALF : (l + 1) * HALF, half]
+                            out=out_view[half, l][:, :, first * D : last * D],
+                            in_=y_sb[l * HALF : (l + 1) * HALF, half, :, 0 : (last - first) * D],
                         )
 
         def is_head(h):
             return 0 <= h < HEADS
 
-        for s in range(-1, HEADS + 3):
-            if is_head(s + LOADS_AHEAD) and s >= 0 and (s + LOADS_AHEAD) % GROUP == 0:
-                load_qk((s + LOADS_AHEAD) // GROUP)
-            if is_head(s + V_LOADS_AHEAD) and s >= 0 and s % V_GROUP == 0:
-                load_v((s + V_LOADS_AHEAD) // V_GROUP)
-            if is_head(s):
-                copy_transposed(s)
-            if s == 0:
-                for h in range(V_GROUP):
-                    regroup_v(h)
+        regroup_v(nc.vector.tensor_copy, 0, v_first[:])
+        for s in range(-1, HEADS + 4):
             if is_head(s - 1):
-                late_bank(s - 1, 0)
-                late_bank(s - 1, 1)
-                early_bank(s - 1)
-            if is_head(s - 2):
-                quantise_sm(s - 2)
+                mixed_bank(s - 1, 0)
+            if s % 2 == 1 and is_head(s - 2):
+                quantise_sm((s - 3) // 2, 0, 4)
+            if is_head(s - 1):
+                mixed_bank(s - 1, 1)
+            if s % 2 == 1 and is_head(s - 2):
+                quantise_sm((s - 3) // 2, 4, 6)
+            if is_head(s - 1):
+                late_bank(s - 1)
             if is_head(s - 1) and (s - 1) % V_GROUP == 0:
                 quantise_v((s - 1) // V_GROUP)
-            if is_head(s - 3):
-                output_head(s - 3)
+                if s == 1:
+                    pair_v(0)
+                    load_v(8, 16)
+                    load_qk(8, 16)
+            if s > 2 and is_head(s - 2) and (s - 2) % V_GROUP == 0:
+                pair_v((s - 2) // V_GROUP)
             if s >= 1 and is_head(s - 1 + V_GROUP):
-                regroup_v(s - 1 + V_GROUP)
+                regroup_v(nc.scalar.copy, s - 1 + V_GROUP, v_sb[s - 1 + V_GROUP])
             if is_head(s):
                 for h in range(s * 2, s * 2 + 2):
                     if is_head(h) and h < TABLES_AHEAD * 2:
@@ -314,3 +316,6 @@ def tile_multiscaleretention_pb_kernel(tc, q_rot, k_rot, v, out):
                     decay_table(s + TABLES_AHEAD)
             if is_head(s + 1):
                 transpose_head(s + 1)
+                copy_transposed(s + 1)
+            if is_head(s - 4):
+                output_head(s - 4)

import math
from contextlib import ExitStack

import concourse.mybir as mybir
from concourse.masks import make_identity

BF16 = mybir.dt.bfloat16
F32 = mybir.dt.float32
U32 = mybir.dt.uint32
I32 = mybir.dt.int32
U8 = mybir.dt.uint8
FP8X4 = mybir.dt.float8_e4m3fn_x4
EXP = mybir.ActivationFunctionType.Exp
MULT = mybir.AluOpType.mult

P = 128
HALF = P // 2
PACK = 4
T = 512
HEADS = 16
D = 128
V_GROUP = 4
V_GROUP_COLS = V_GROUP * D
STORES = ((0, 4), (4, 8), (8, 12), (12, 14), (14, 15), (15, 16))
STORE_COLS = 4 * D
MASKED = 2.0 ** 30
V_RUN = 4
SM_BLOCKS = 3
SM_BUFS = 3
PAD_BUFS = 3
TABLES_AHEAD = 4
DECAY_COLS = T // 2 + PACK

FLOPS = 2 * 2 * HEADS * T * T * D


def tile_multiscaleretention_pb_kernel(tc, q_rot, k_rot, v, out):
    nc = tc.nc
    q_view = q_rot.rearrange("b (p c) e -> p (b c) e", c=PACK)
    k_view = k_rot.rearrange("b (p c) e -> p (b c) e", c=PACK)
    v_view = v.rearrange("b (p c) e -> p (b c) e", c=PACK)
    out_view = out.rearrange("b (h i c l) e -> h l i (b c) e", h=2, c=2, l=2)

    with ExitStack() as ctx:
        ctx.enter_context(tc.manual_schedule())
        keep = ctx.enter_context(tc.tile_pool(name="keep", bufs=1))
        work = ctx.enter_context(tc.tile_pool(name="work", bufs=3))
        psum_t = ctx.enter_context(tc.psum_pool(name="psum_t", bufs=2))
        psum_s = ctx.enter_context(tc.psum_pool(name="psum_s", bufs=4))
        psum_y = ctx.enter_context(tc.psum_pool(name="psum_y", bufs=2))

        q_sb = {}
        k_sb = {}
        v_sb = {}

        def load(source, view, tiles, first, last):
            tile = keep.tile([P, PACK, (last - first) * D], BF16, name="%s_%d" % (source, first))
            nc.sync.dma_start(out=tile[:], in_=view[:, :, first * D : last * D])
            for h in range(first, last):
                tiles[h] = tile[:, :, (h - first) * D : (h - first + 1) * D]
            return tile

        def load_qk(first, last):
            load("q", q_view, q_sb, first, last)
            load("k", k_view, k_sb, first, last)

        def load_v(first, last):
            return load("v", v_view, v_sb, first, last)

        load_qk(0, 2)
        v_first = load_v(0, 4)
        load_qk(2, 4)
        load_v(4, 8)
        load_qk(4, 8)

        ident = keep.tile([P, P], BF16, name="ident")
        make_identity(nc, ident[:])
        distance = keep.tile([P, 2, DECAY_COLS], F32, name="distance")

        def fill_distance(part, base):
            pattern = [[1, DECAY_COLS]]
            nc.gpsimd.iota(
                part, pattern=pattern, base=base, channel_multiplier=-PACK, allow_small_or_imprecise_dtypes=True
            )
            nc.gpsimd.affine_select(
                out=part,
                in_=part,
                pattern=pattern,
                compare_op=mybir.AluOpType.is_ge,
                fill=MASKED,
                base=base,
                channel_multiplier=-PACK,
            )

        fill_distance(distance[:, 0], T // 2 - 3)
        fill_distance(distance[0:HALF, 1], -3)
        fill_distance(distance[HALF:P, 1], -1)

        k_pads = []
        for i in range(PAD_BUFS):
            k_pad = keep.tile([P, PACK, 3 * HALF], BF16, name="k_pad_%d" % i)
            nc.vector.memset(k_pad[:].bitcast(U32), 0)
            k_pads.append(k_pad)

        sm_tiles = []
        for i in range(SM_BUFS):
            sm_i = keep.tile([P, 2, SM_BLOCKS, P, PACK], BF16, name="sm_%d" % i, align_bytes=64)
            sm_tiles.append(sm_i)

        v_codes = keep.tile([P, HEADS * D], U32, name="v_codes", align_bytes=64)
        v_scales = keep.tile([P, HEADS * D], U8, name="v_scales", align_bytes=64)
        nc.vector.memset(v_scales[:].bitcast(U32), 0)
        v_pair_codes = []
        v_pair_scales = []
        for g in range(HEADS // V_GROUP):
            codes_g = keep.tile([P, V_GROUP, 2, D], U32, name="v_pair_codes_%d" % g, align_bytes=64)
            scales_g = keep.tile([P, V_GROUP, 2, D], U8, name="v_pair_scales_%d" % g, align_bytes=64)
            zeroing = nc.vector if g < 2 else nc.gpsimd
            zeroing.memset(codes_g[:], 0)
            zeroing.memset(scales_g[:].bitcast(U32), 0)
            v_pair_codes.append(codes_g)
            v_pair_scales.append(scales_g)

        qk_banks = {}
        qk_ts = {}
        decays = {}
        v_groupeds = {}
        sm_quantised = {}
        y_sbs = {}

        def decay_table(h):
            decay = keep.tile([P, 2, DECAY_COLS], F32, name="decay_%d" % h)
            nc.scalar.activation(
                out=decay[:],
                in_=distance[:],
                func=EXP,
                scale=math.log(1.0 - 2.0 ** (-5 - h)),
                bias=-0.5 * math.log(D),
            )
            decays[h] = decay

        def transpose_head(h):
            qk_ps = psum_t.tile([P, 2 * PACK, P], BF16)
            for c in range(PACK):
                nc.tensor.transpose(qk_ps[:, c, :], q_sb[h][:, c, :], ident[:])
            for c in range(PACK):
                nc.tensor.transpose(qk_ps[:, PACK + c, :], k_sb[h][:, c, :], ident[:])
            qk_banks[h] = qk_ps

        def copy_transposed(h):
            qk_t = work.tile([P, 2 * PACK, P], BF16)
            nc.scalar.copy(out=qk_t[:].bitcast(F32), in_=qk_banks[h][:].bitcast(F32))
            nc.scalar.copy(
                out=k_pads[h % PAD_BUFS][:, :, HALF:P].bitcast(F32), in_=qk_banks[h][:, PACK:, 0:HALF].bitcast(F32)
            )
            qk_ts[h] = qk_t

        def key_slot(h, r):
            return qk_ts[h][:, 2 * PACK - 1 - r, :]

        def mixed_bank(h, l):
            qk_t = qk_ts[h]
            k_pad = k_pads[h % PAD_BUFS]
            s_ps = psum_s.tile([P, PACK, 2, HALF], F32, tag="s_ps")
            for r in range(PACK):
                slot = PACK - 1 - r
                nc.tensor.matmul(
                    out=s_ps[:, r, 0], lhsT=key_slot(h, r), rhs=qk_t[:, l, HALF:P], start=True, stop=True
                )
                nc.tensor.matmul(
                    out=s_ps[:, r, 1], lhsT=k_pad[:, slot, HALF:], rhs=qk_t[:, l, 0:HALF], start=True, stop=False
                )
                nc.tensor.matmul(
                    out=s_ps[:, r, 1], lhsT=k_pad[:, slot, 0:P], rhs=qk_t[:, l + 2, 0:HALF], start=False, stop=True
                )
            nc.vector.tensor_tensor(
                out=sm_tiles[h // 2 % SM_BUFS][:, h % 2, 0:3:2, l * HALF : (l + 1) * HALF, :],
                in0=s_ps[:].rearrange("p r b i -> p b i r"),
                in1=decays[h][:, :, l : l + T // 2].rearrange("p b (i r) -> p b i r", r=PACK),
                op=MULT,
            )

        def late_bank(h):
            qk_t = qk_ts[h]
            s_ps = psum_s.tile([P, PACK, 2, HALF], F32, tag="s_ps")
            for r in range(PACK):
                nc.tensor.matmul(
                    out=s_ps[:, r], lhsT=key_slot(h, r), rhs=qk_t[:, 2:4, HALF:P], start=True, stop=True
                )
            for l in range(2):
                nc.vector.tensor_tensor(
                    out=sm_tiles[h // 2 % SM_BUFS][:, h % 2, 1, l * HALF : (l + 1) * HALF, :],
                    in0=s_ps[:, :, l, :].rearrange("p r i -> p i r"),
                    in1=decays[h][:, 0, 2 + l : 2 + l + T // 2].rearrange("p (i r) -> p i r", r=PACK),
                    op=MULT,
                )

        def quantise_sm(pair, first, last):
            if first == 0:
                sm_codes = work.tile([P, 2 * SM_BLOCKS * P], U32, align_bytes=64)
                sm_scales = work.tile([P, 2 * SM_BLOCKS * P], U8, align_bytes=64)
                sm_quantised[pair] = (sm_codes, sm_scales)
            sm_codes, sm_scales = sm_quantised[pair]
            cols = slice(first * P, last * P)
            nc.vector.quantize_mx(
                out=sm_codes[:, cols].bitcast(FP8X4),
                scales=sm_scales[:, cols],
                in_=sm_tiles[pair % SM_BUFS][:].rearrange("p h b m r -> p (h b m r)")[
                    :, first * P * PACK : last * P * PACK
                ],
            )

        def regroup_v(copy, h, source):
            g = h // V_GROUP
            if h % V_GROUP == 0:
                v_groupeds[g] = work.tile([P, V_GROUP_COLS, PACK], BF16, name="v_grouped", align_bytes=64, bufs=2)
            cols = slice((h % V_GROUP) * D, (h % V_GROUP) * D + source.shape[2])
            copy(
                out=v_groupeds[g][:, cols, :].rearrange("p (e i) r -> p e r i", i=V_RUN),
                in_=source[:, ::-1, :].rearrange("p r (e i) -> p e r i", i=V_RUN),
            )

        def quantise_v(g):
            cols = slice(g * V_GROUP_COLS, (g + 1) * V_GROUP_COLS)
            nc.vector.quantize_mx(
                out=v_codes[:, cols].bitcast(FP8X4),
                scales=v_scales[:, cols],
                in_=v_groupeds[g][:].rearrange("p e r -> p (e r)"),
            )

        def pair_v(g):
            cols = slice(g * V_GROUP_COLS, (g + 1) * V_GROUP_COLS)
            for half in range(2):
                rows = slice(half * HALF, (half + 1) * HALF)
                nc.sync.dma_start(
                    out=v_pair_codes[g][rows, :, half, :].bitcast(I32),
                    in_=v_codes[0:HALF, cols].bitcast(I32).rearrange("p (h e) -> p h e", h=V_GROUP),
                )
                nc.sync.dma_start(
                    out=v_pair_scales[g][rows, :, half, :].bitcast(I32),
                    in_=v_scales[0:HALF, cols].bitcast(I32).rearrange("p (h e) -> p h e", h=V_GROUP),
                )

        def output_head(h):
            sm_codes, sm_scales = sm_quantised[h // 2]
            block = (h % 2) * SM_BLOCKS
            cols = slice(h * D, (h + 1) * D)
            g = h // V_GROUP
            pair_codes = v_pair_codes[g][:, h % V_GROUP].rearrange("p a e -> p (a e)")
            pair_scales = v_pair_scales[g][:, h % V_GROUP].rearrange("p a e -> p (a e)")
            y_ps = psum_y.tile([P, 2, 2, D], F32)
            for b in range(2):
                rows = slice((block + b) * P, (block + b + 1) * P)
                nc.tensor.matmul_mx(
                    out=y_ps[:, 1, b, :],
                    lhsT=sm_codes[:, rows].bitcast(FP8X4),
                    lhsT_scale=sm_scales[:, rows],
                    rhs=v_codes[:, cols].bitcast(FP8X4),
                    rhs_scale=v_scales[:, cols],
                    start=True,
                    stop=True,
                )
            rows = slice((block + 2) * P, (block + 3) * P)
            nc.tensor.matmul_mx(
                out=y_ps[:, 0].rearrange("p c e -> p (c e)"),
                lhsT=sm_codes[:, rows].bitcast(FP8X4),
                lhsT_scale=sm_scales[:, rows],
                rhs=pair_codes.bitcast(FP8X4),
                rhs_scale=pair_scales,
                start=True,
                stop=True,
            )
            first, last = [store for store in STORES if store[0] <= h < store[1]][0]
            if h == first:
                y_sbs[first] = work.tile([P, 2, 2, STORE_COLS], F32, name="y_sb")
            y_sb = y_sbs[first]
            nc.scalar.copy(out=y_sb[:, :, :, (h - first) * D : (h - first + 1) * D], in_=y_ps[:])
            if h == last - 1:
                for half in range(2):
                    for l in range(2):
                        nc.sync.dma_start(
                            out=out_view[half, l][:, :, first * D : last * D],
                            in_=y_sb[l * HALF : (l + 1) * HALF, half, :, 0 : (last - first) * D],
                        )

        def is_head(h):
            return 0 <= h < HEADS

        regroup_v(nc.vector.tensor_copy, 0, v_first[:])
        for s in range(-1, HEADS + 4):
            if is_head(s - 1):
                mixed_bank(s - 1, 0)
            if s % 2 == 1 and is_head(s - 2):
                quantise_sm((s - 3) // 2, 0, 4)
            if is_head(s - 1):
                mixed_bank(s - 1, 1)
            if s % 2 == 1 and is_head(s - 2):
                quantise_sm((s - 3) // 2, 4, 6)
            if is_head(s - 1):
                late_bank(s - 1)
            if is_head(s - 1) and (s - 1) % V_GROUP == 0:
                quantise_v((s - 1) // V_GROUP)
                if s == 1:
                    pair_v(0)
                    load_v(8, 16)
                    load_qk(8, 16)
            if s > 2 and is_head(s - 2) and (s - 2) % V_GROUP == 0:
                pair_v((s - 2) // V_GROUP)
            if s >= 1 and is_head(s - 1 + V_GROUP):
                regroup_v(nc.scalar.copy, s - 1 + V_GROUP, v_sb[s - 1 + V_GROUP])
            if is_head(s):
                for h in range(s * 2, s * 2 + 2):
                    if is_head(h) and h < TABLES_AHEAD * 2:
                        decay_table(h)
                if s >= TABLES_AHEAD and is_head(s + TABLES_AHEAD):
                    decay_table(s + TABLES_AHEAD)
            if is_head(s + 1):
                transpose_head(s + 1)
                copy_transposed(s + 1)
            if is_head(s - 4):
                output_head(s - 4)
